import numpy as np
import ml_dtypes

BF16 = ml_dtypes.bfloat16


def bf(x):
    return np.asarray(x, np.float32).astype(BF16)


def f32(x):
    return np.asarray(x, np.float32)


def f64(x):
    return np.asarray(x).astype(np.float64)


def striped(idx):
    return np.tile(idx.reshape(-1, 16).T, (8, 1))


C, F, S, N = 128, 512, 1024, 256
RW = 0.25


def setup_inputs():
    return {"base": f32(np.random.standard_normal((C, S))), "h": f32(np.random.standard_normal((C, N))), "w1": bf(np.random.standard_normal((C, F)) / np.sqrt(C)), "w2": bf(np.random.standard_normal((F, C)) / np.sqrt(F)), "offs": striped(np.random.permutation(S)[:N])}


def reference(base, h, w1, w2, offs):
    idx = offs[:16].T.reshape(-1)
    hid = np.maximum(f64(w1).T @ f64(h), 0.0)
    u = RW * (f64(w2).T @ hid)
    out = f64(base).copy()
    out[:, idx] = f64(h) + u
    return out

@@ -1,0 +1,54 @@
+import concourse.mybir as mybir
+
+F32, BF16, U16 = mybir.dt.float32, mybir.dt.bfloat16, mybir.dt.uint16
+ALU = mybir.AluOpType
+RELU = mybir.ActivationFunctionType.Relu
+
+C, F, S, N = 128, 512, 1024, 256
+P = 128
+FB = F // P
+RW = 0.25
+
+FLOPS = 2 * C * F * N * 2
+
+
+def tile_cosformermodel_kernel(tc, base, h, w1, w2, offs, out):
+    nc = tc.nc
+    with (
+        tc.tile_pool(name="held", bufs=1) as held,
+        tc.psum_pool(name="psum", bufs=1) as psum,
+    ):
+        h_f32 = held.tile([C, N], F32, name="h_f32")
+        nc.sync.dma_start(h_f32[:], h)
+        w1_sb = held.tile([C, F], BF16, name="w1_sb")
+        nc.scalar.dma_start(w1_sb[:], w1)
+        offsets = held.tile([P, N // 16], U16, name="offsets")
+        nc.sync.dma_start(offsets[:], offs)
+        w2_sb = held.tile([P, FB, C], BF16, name="w2_sb")
+        nc.scalar.dma_start(w2_sb[:], w2.rearrange("(k p) c -> p k c", p=P))
+        window = held.tile([C, S], F32, name="window")
+        nc.sync.dma_start(window[:], base)
+
+        h_bf = held.tile([C, N], BF16, name="h_bf")
+        nc.vector.tensor_copy(h_bf[:], h_f32[:])
+
+        hid_bf = []
+        for k in range(FB):
+            hid_ps = psum.tile([P, N], F32, name=f"hid_ps{k}")
+            nc.tensor.matmul(hid_ps[:], w1_sb[:, k * P : (k + 1) * P], h_bf[:], start=True, stop=True)
+            hid_k = held.tile([P, N], BF16, name=f"hid_bf{k}")
+            if k % 2 == 0:
+                nc.scalar.activation(hid_k[:], hid_ps[:], RELU)
+            else:
+                nc.vector.tensor_scalar_max(hid_k[:], hid_ps[:], 0.0)
+            hid_bf.append(hid_k)
+
+        u_ps = psum.tile([C, N], F32, name="u_ps")
+        for k in range(FB):
+            nc.tensor.matmul(u_ps[:], w2_sb[:, k, :], hid_bf[k][:], start=(k == 0), stop=(k == FB - 1))
+
+        u_sb = held.tile([C, N], F32, name="u_sb")
+        nc.vector.tensor_scalar_mul(u_sb[:], u_ps[:], RW)
+
+        nc.vector.tensor_tensor(window[:].indirect(offsets[:]), h_f32[:], u_sb[:], ALU.add)
+        nc.sync.dma_start(out, window[:])

@@ -8,6 +8,8 @@ C, F, S, N = 128, 512, 1024, 256
 P = 128
 FB = F // P
 RW = 0.25
+BANK = 512
+WARM_UPS = 5
 
 FLOPS = 2 * C * F * N * 2
 
@@ -18,6 +20,12 @@ def tile_cosformermodel_kernel(tc, base, h, w1, w2, offs, out):
         tc.tile_pool(name="held", bufs=1) as held,
         tc.psum_pool(name="psum", bufs=1) as psum,
     ):
+        zeros = held.tile([P, BANK], BF16, name="zeros")
+        nc.vector.memset(zeros[:], 0.0)
+        warm_ps = psum.tile([P, BANK], F32, name="warm_ps")
+        for i in range(WARM_UPS):
+            nc.tensor.matmul(warm_ps[:], zeros[:, :P], zeros[:], start=True, stop=True)
+
         h_f32 = held.tile([C, N], F32, name="h_f32")
         nc.sync.dma_start(h_f32[:], h)
         w1_sb = held.tile([C, F], BF16, name="w1_sb")

@@ -8,8 +8,6 @@ C, F, S, N = 128, 512, 1024, 256
 P = 128
 FB = F // P
 RW = 0.25
-BANK = 512
-WARM_UPS = 5
 
 FLOPS = 2 * C * F * N * 2
 
@@ -20,12 +18,6 @@ def tile_cosformermodel_kernel(tc, base, h, w1, w2, offs, out):
         tc.tile_pool(name="held", bufs=1) as held,
         tc.psum_pool(name="psum", bufs=1) as psum,
     ):
-        zeros = held.tile([P, BANK], BF16, name="zeros")
-        nc.vector.memset(zeros[:], 0.0)
-        warm_ps = psum.tile([P, BANK], F32, name="warm_ps")
-        for i in range(WARM_UPS):
-            nc.tensor.matmul(warm_ps[:], zeros[:, :P], zeros[:], start=True, stop=True)
-
         h_f32 = held.tile([C, N], F32, name="h_f32")
         nc.sync.dma_start(h_f32[:], h)
         w1_sb = held.tile([C, F], BF16, name="w1_sb")
@@ -59,4 +51,5 @@ def tile_cosformermodel_kernel(tc, base, h, w1, w2, offs, out):
         nc.vector.tensor_scalar_mul(u_sb[:], u_ps[:], RW)
 
         nc.vector.tensor_tensor(window[:].indirect(offsets[:]), h_f32[:], u_sb[:], ALU.add)
-        nc.sync.dma_start(out, window[:])
+        nc.sync.dma_start(out[:, : S // 2], window[:, : S // 2])
+        nc.scalar.dma_start(out[:, S // 2 :], window[:, S // 2 :])

@@ -21,11 +21,11 @@ def tile_cosformermodel_kernel(tc, base, h, w1, w2, offs, out):
         h_f32 = held.tile([C, N], F32, name="h_f32")
         nc.sync.dma_start(h_f32[:], h)
         w1_sb = held.tile([C, F], BF16, name="w1_sb")
-        nc.scalar.dma_start(w1_sb[:], w1)
+        nc.sync.dma_start(w1_sb[:], w1)
+        w2_sb = held.tile([P, FB, C], BF16, name="w2_sb")
+        nc.sync.dma_start(w2_sb[:], w2.rearrange("(k p) c -> p k c", p=P))
         offsets = held.tile([P, N // 16], U16, name="offsets")
         nc.sync.dma_start(offsets[:], offs)
-        w2_sb = held.tile([P, FB, C], BF16, name="w2_sb")
-        nc.scalar.dma_start(w2_sb[:], w2.rearrange("(k p) c -> p k c", p=P))
         window = held.tile([C, S], F32, name="window")
         nc.sync.dma_start(window[:], base)
 
@@ -51,5 +51,4 @@ def tile_cosformermodel_kernel(tc, base, h, w1, w2, offs, out):
         nc.vector.tensor_scalar_mul(u_sb[:], u_ps[:], RW)
 
         nc.vector.tensor_tensor(window[:].indirect(offsets[:]), h_f32[:], u_sb[:], ALU.add)
-        nc.sync.dma_start(out[:, : S // 2], window[:, : S // 2])
-        nc.scalar.dma_start(out[:, S // 2 :], window[:, S // 2 :])
+        nc.sync.dma_start(out, window[:])

@@ -8,6 +8,8 @@ C, F, S, N = 128, 512, 1024, 256
 P = 128
 FB = F // P
 RW = 0.25
+BANK = 512
+WARM_UPS = 4
 
 FLOPS = 2 * C * F * N * 2
 
@@ -18,6 +20,18 @@ def tile_cosformermodel_kernel(tc, base, h, w1, w2, offs, out):
         tc.tile_pool(name="held", bufs=1) as held,
         tc.psum_pool(name="psum", bufs=1) as psum,
     ):
+        zeros = held.tile([P, P], BF16, name="zeros")
+        nc.vector.memset(zeros[:], 0.0)
+        warm_ps = psum.tile([P, BANK], F32, name="warm_ps")
+        for i in range(WARM_UPS):
+            nc.tensor.matmul(
+                warm_ps[:].rearrange("p (r c) -> p r c", c=P),
+                zeros[:],
+                zeros[:].unsqueeze(1).to_broadcast([P, BANK // P, P]),
+                start=True,
+                stop=True,
+            )
+
         h_f32 = held.tile([C, N], F32, name="h_f32")
         nc.sync.dma_start(h_f32[:], h)
         w1_sb = held.tile([C, F], BF16, name="w1_sb")

@@ -9,7 +9,7 @@ P = 128
 FB = F // P
 RW = 0.25
 BANK = 512
-WARM_UPS = 4
+WARM_UPS = 3
 
 FLOPS = 2 * C * F * N * 2
 

@@ -2,7 +2,6 @@ import concourse.mybir as mybir
 
 F32, BF16, U16 = mybir.dt.float32, mybir.dt.bfloat16, mybir.dt.uint16
 ALU = mybir.AluOpType
-RELU = mybir.ActivationFunctionType.Relu
 
 C, F, S, N = 128, 512, 1024, 256
 P = 128
@@ -48,13 +47,10 @@ def tile_cosformermodel_kernel(tc, base, h, w1, w2, offs, out):
 
         hid_bf = []
         for k in range(FB):
-            hid_ps = psum.tile([P, N], F32, name=f"hid_ps{k}")
+            hid_ps = psum.tile([P, N], BF16, name=f"hid_ps{k}")
             nc.tensor.matmul(hid_ps[:], w1_sb[:, k * P : (k + 1) * P], h_bf[:], start=True, stop=True)
             hid_k = held.tile([P, N], BF16, name=f"hid_bf{k}")
-            if k % 2 == 0:
-                nc.scalar.activation(hid_k[:], hid_ps[:], RELU)
-            else:
-                nc.vector.tensor_scalar_max(hid_k[:], hid_ps[:], 0.0)
+            nc.vector.tensor_scalar_max(hid_k[:], hid_ps[:], 0.0)
             hid_bf.append(hid_k)
 
         u_ps = psum.tile([C, N], F32, name="u_ps")

@@ -2,12 +2,14 @@ import concourse.mybir as mybir
 
 F32, BF16, U16 = mybir.dt.float32, mybir.dt.bfloat16, mybir.dt.uint16
 ALU = mybir.AluOpType
+COPY = mybir.ActivationFunctionType.Copy
 
 C, F, S, N = 128, 512, 1024, 256
 P = 128
 FB = F // P
 RW = 0.25
 BANK = 512
+HALF = N // 2
 WARM_UPS = 3
 
 FLOPS = 2 * C * F * N * 2
@@ -53,12 +55,20 @@ def tile_cosformermodel_kernel(tc, base, h, w1, w2, offs, out):
             nc.vector.tensor_scalar_max(hid_k[:], hid_ps[:], 0.0)
             hid_bf.append(hid_k)
 
-        u_ps = psum.tile([C, N], F32, name="u_ps")
+        u_ps = [psum.tile([C, HALF], F32, name=f"u_ps{t}") for t in range(2)]
         for k in range(FB):
-            nc.tensor.matmul(u_ps[:], w2_sb[:, k, :], hid_bf[k][:], start=(k == 0), stop=(k == FB - 1))
+            for t in range(2):
+                nc.tensor.matmul(
+                    u_ps[t][:],
+                    w2_sb[:, k, :],
+                    hid_bf[k][:, t * HALF : (t + 1) * HALF],
+                    start=(k == 0),
+                    stop=(k == FB - 1),
+                )
 
         u_sb = held.tile([C, N], F32, name="u_sb")
-        nc.vector.tensor_scalar_mul(u_sb[:], u_ps[:], RW)
+        nc.vector.tensor_scalar_mul(u_sb[:, 0:HALF], u_ps[0][:], RW)
+        nc.scalar.activation(u_sb[:, HALF:N], u_ps[1][:], COPY, scale=RW)
 
         nc.vector.tensor_tensor(window[:].indirect(offsets[:]), h_f32[:], u_sb[:], ALU.add)
         nc.sync.dma_start(out, window[:])

@@ -2,7 +2,6 @@ import concourse.mybir as mybir
 
 F32, BF16, U16 = mybir.dt.float32, mybir.dt.bfloat16, mybir.dt.uint16
 ALU = mybir.AluOpType
-COPY = mybir.ActivationFunctionType.Copy
 
 C, F, S, N = 128, 512, 1024, 256
 P = 128
@@ -11,6 +10,7 @@ RW = 0.25
 BANK = 512
 HALF = N // 2
 WARM_UPS = 3
+WARM_COLS = 32
 
 FLOPS = 2 * C * F * N * 2
 
@@ -21,14 +21,14 @@ def tile_cosformermodel_kernel(tc, base, h, w1, w2, offs, out):
         tc.tile_pool(name="held", bufs=1) as held,
         tc.psum_pool(name="psum", bufs=1) as psum,
     ):
-        zeros = held.tile([P, P], BF16, name="zeros")
+        zeros = held.tile([P, WARM_COLS], BF16, name="zeros")
         nc.vector.memset(zeros[:], 0.0)
-        warm_ps = psum.tile([P, BANK], F32, name="warm_ps")
+        warm_ps = psum.tile([WARM_COLS, BANK], F32, name="warm_ps")
         for i in range(WARM_UPS):
             nc.tensor.matmul(
-                warm_ps[:].rearrange("p (r c) -> p r c", c=P),
+                warm_ps[:].rearrange("p (r c) -> p r c", c=WARM_COLS),
                 zeros[:],
-                zeros[:].unsqueeze(1).to_broadcast([P, BANK // P, P]),
+                zeros[:].unsqueeze(1).to_broadcast([P, BANK // WARM_COLS, WARM_COLS]),
                 start=True,
                 stop=True,
             )
@@ -49,10 +49,14 @@ def tile_cosformermodel_kernel(tc, base, h, w1, w2, offs, out):
 
         hid_bf = []
         for k in range(FB):
-            hid_ps = psum.tile([P, N], BF16, name=f"hid_ps{k}")
-            nc.tensor.matmul(hid_ps[:], w1_sb[:, k * P : (k + 1) * P], h_bf[:], start=True, stop=True)
             hid_k = held.tile([P, N], BF16, name=f"hid_bf{k}")
-            nc.vector.tensor_scalar_max(hid_k[:], hid_ps[:], 0.0)
+            width = HALF if k == FB - 1 else N
+            for j in range(0, N, width):
+                hid_ps = psum.tile([P, width], BF16, name=f"hid_ps{k}_{j}")
+                nc.tensor.matmul(
+                    hid_ps[:], w1_sb[:, k * P : (k + 1) * P], h_bf[:, j : j + width], start=True, stop=True
+                )
+                nc.vector.tensor_scalar_max(hid_k[:, j : j + width], hid_ps[:], 0.0)
             hid_bf.append(hid_k)
 
         u_ps = [psum.tile([C, HALF], F32, name=f"u_ps{t}") for t in range(2)]
@@ -67,8 +71,8 @@ def tile_cosformermodel_kernel(tc, base, h, w1, w2, offs, out):
                 )
 
         u_sb = held.tile([C, N], F32, name="u_sb")
-        nc.vector.tensor_scalar_mul(u_sb[:, 0:HALF], u_ps[0][:], RW)
-        nc.scalar.activation(u_sb[:, HALF:N], u_ps[1][:], COPY, scale=RW)
+        for t in range(2):
+            nc.vector.tensor_scalar_mul(u_sb[:, t * HALF : (t + 1) * HALF], u_ps[t][:], RW)
 
         nc.vector.tensor_tensor(window[:].indirect(offsets[:]), h_f32[:], u_sb[:], ALU.add)
         nc.sync.dma_start(out, window[:])

@@ -45,30 +45,44 @@ def tile_cosformermodel_kernel(tc, base, h, w1, w2, offs, out):
         nc.sync.dma_start(window[:], base)
 
         h_bf = held.tile([C, N], BF16, name="h_bf")
-        nc.vector.tensor_copy(h_bf[:], h_f32[:])
+        for j in range(0, N, HALF):
+            nc.vector.tensor_copy(h_bf[:, j : j + HALF], h_f32[:, j : j + HALF])
 
         hid_bf = []
         for k in range(FB):
             hid_k = held.tile([P, N], BF16, name=f"hid_bf{k}")
-            width = HALF if k == FB - 1 else N
-            for j in range(0, N, width):
-                hid_ps = psum.tile([P, width], BF16, name=f"hid_ps{k}_{j}")
-                nc.tensor.matmul(
-                    hid_ps[:], w1_sb[:, k * P : (k + 1) * P], h_bf[:, j : j + width], start=True, stop=True
-                )
-                nc.vector.tensor_scalar_max(hid_k[:, j : j + width], hid_ps[:], 0.0)
+            relu_width = HALF if k == FB - 1 else N
+            matmul_width = HALF if k in (0, FB - 1) else N
+            for j in range(0, N, relu_width):
+                hid_ps = psum.tile([P, relu_width], BF16, name=f"hid_ps{k}_{j}")
+                for i in range(0, relu_width, matmul_width):
+                    nc.tensor.matmul(
+                        hid_ps[:, i : i + matmul_width],
+                        w1_sb[:, k * P : (k + 1) * P],
+                        h_bf[:, j + i : j + i + matmul_width],
+                        start=True,
+                        stop=True,
+                    )
+                nc.vector.tensor_scalar_max(hid_k[:, j : j + relu_width], hid_ps[:], 0.0)
             hid_bf.append(hid_k)
 
         u_ps = [psum.tile([C, HALF], F32, name=f"u_ps{t}") for t in range(2)]
-        for k in range(FB):
+
+        def add_block(k, t):
+            nc.tensor.matmul(
+                u_ps[t][:],
+                w2_sb[:, k, :],
+                hid_bf[k][:, t * HALF : (t + 1) * HALF],
+                start=(k == 0),
+                stop=(k == FB - 1),
+            )
+
+        for k in range(FB - 2):
             for t in range(2):
-                nc.tensor.matmul(
-                    u_ps[t][:],
-                    w2_sb[:, k, :],
-                    hid_bf[k][:, t * HALF : (t + 1) * HALF],
-                    start=(k == 0),
-                    stop=(k == FB - 1),
-                )
+                add_block(k, t)
+        for t in range(2):
+            for k in range(FB - 2, FB):
+                add_block(k, t)
 
         u_sb = held.tile([C, N], F32, name="u_sb")
         for t in range(2):

@@ -35,10 +35,10 @@ def tile_cosformermodel_kernel(tc, base, h, w1, w2, offs, out):
 
         h_f32 = held.tile([C, N], F32, name="h_f32")
         nc.sync.dma_start(h_f32[:], h)
-        w1_sb = held.tile([C, F], BF16, name="w1_sb")
-        nc.sync.dma_start(w1_sb[:], w1)
+        w1_sb = held.tile([C, P, FB], BF16, name="w1_sb")
+        nc.sync.dma_start(w1_sb[:], w1.rearrange("c (p k) -> c p k", k=FB))
         w2_sb = held.tile([P, FB, C], BF16, name="w2_sb")
-        nc.sync.dma_start(w2_sb[:], w2.rearrange("(k p) c -> p k c", p=P))
+        nc.sync.dma_start(w2_sb[:], w2.rearrange("(p k) c -> p k c", k=FB))
         offsets = held.tile([P, N // 16], U16, name="offsets")
         nc.sync.dma_start(offsets[:], offs)
         window = held.tile([C, S], F32, name="window")
@@ -58,7 +58,7 @@ def tile_cosformermodel_kernel(tc, base, h, w1, w2, offs, out):
                 for i in range(0, relu_width, matmul_width):
                     nc.tensor.matmul(
                         hid_ps[:, i : i + matmul_width],
-                        w1_sb[:, k * P : (k + 1) * P],
+                        w1_sb[:, :, k],
                         h_bf[:, j + i : j + i + matmul_width],
                         start=True,
                         stop=True,

@@ -23,7 +23,7 @@ def tile_cosformermodel_kernel(tc, base, h, w1, w2, offs, out):
     ):
         zeros = held.tile([P, WARM_COLS], BF16, name="zeros")
         nc.vector.memset(zeros[:], 0.0)
-        warm_ps = psum.tile([WARM_COLS, BANK], F32, name="warm_ps")
+        warm_ps = psum.tile([WARM_COLS, BANK], F32, name="warm_ps", tag="u_ps0")
         for i in range(WARM_UPS):
             nc.tensor.matmul(
                 warm_ps[:].rearrange("p (r c) -> p r c", c=WARM_COLS),
@@ -48,23 +48,25 @@ def tile_cosformermodel_kernel(tc, base, h, w1, w2, offs, out):
         for j in range(0, N, HALF):
             nc.vector.tensor_copy(h_bf[:, j : j + HALF], h_f32[:, j : j + HALF])
 
-        hid_bf = []
-        for k in range(FB):
-            hid_k = held.tile([P, N], BF16, name=f"hid_bf{k}")
-            relu_width = HALF if k == FB - 1 else N
-            matmul_width = HALF if k in (0, FB - 1) else N
-            for j in range(0, N, relu_width):
-                hid_ps = psum.tile([P, relu_width], BF16, name=f"hid_ps{k}_{j}")
-                for i in range(0, relu_width, matmul_width):
-                    nc.tensor.matmul(
-                        hid_ps[:, i : i + matmul_width],
-                        w1_sb[:, :, k],
-                        h_bf[:, j + i : j + i + matmul_width],
-                        start=True,
-                        stop=True,
-                    )
-                nc.vector.tensor_scalar_max(hid_k[:, j : j + relu_width], hid_ps[:], 0.0)
-            hid_bf.append(hid_k)
+        hid_bf = [held.tile([P, N], BF16, name=f"hid_bf{k}") for k in range(FB)]
+
+        def relu_of_product(k, start, end, matmul_width):
+            hid_ps = psum.tile([P, end - start], BF16, name=f"hid_ps{k}_{start}")
+            for j in range(start, end, matmul_width):
+                nc.tensor.matmul(
+                    hid_ps[:, j - start : j - start + matmul_width],
+                    w1_sb[:, :, k],
+                    h_bf[:, j : j + matmul_width],
+                    start=True,
+                    stop=True,
+                )
+            nc.vector.tensor_scalar_max(hid_bf[k][:, start:end], hid_ps[:], 0.0)
+
+        relu_of_product(0, 0, N, HALF)
+        relu_of_product(1, 0, N, N)
+        for t in range(2):
+            for k in range(2, FB):
+                relu_of_product(k, t * HALF, (t + 1) * HALF, HALF)
 
         u_ps = [psum.tile([C, HALF], F32, name=f"u_ps{t}") for t in range(2)]
 
@@ -77,11 +79,11 @@ def tile_cosformermodel_kernel(tc, base, h, w1, w2, offs, out):
                 stop=(k == FB - 1),
             )
 
-        for k in range(FB - 2):
+        for k in range(2):
             for t in range(2):
                 add_block(k, t)
         for t in range(2):
-            for k in range(FB - 2, FB):
+            for k in range(2, FB):
                 add_block(k, t)
 
         u_sb = held.tile([C, N], F32, name="u_sb")

import concourse.mybir as mybir

F32, BF16, U16 = mybir.dt.float32, mybir.dt.bfloat16, mybir.dt.uint16
ALU = mybir.AluOpType

C, F, S, N = 128, 512, 1024, 256
P = 128
FB = F // P
RW = 0.25
BANK = 512
HALF = N // 2
WARM_UPS = 3
WARM_COLS = 32

FLOPS = 2 * C * F * N * 2


def tile_cosformermodel_kernel(tc, base, h, w1, w2, offs, out):
    nc = tc.nc
    with (
        tc.tile_pool(name="held", bufs=1) as held,
        tc.psum_pool(name="psum", bufs=1) as psum,
    ):
        zeros = held.tile([P, WARM_COLS], BF16, name="zeros")
        nc.vector.memset(zeros[:], 0.0)
        warm_ps = psum.tile([WARM_COLS, BANK], F32, name="warm_ps", tag="u_ps0")
        for i in range(WARM_UPS):
            nc.tensor.matmul(
                warm_ps[:].rearrange("p (r c) -> p r c", c=WARM_COLS),
                zeros[:],
                zeros[:].unsqueeze(1).to_broadcast([P, BANK // WARM_COLS, WARM_COLS]),
                start=True,
                stop=True,
            )

        h_f32 = held.tile([C, N], F32, name="h_f32")
        nc.sync.dma_start(h_f32[:], h)
        w1_sb = held.tile([C, P, FB], BF16, name="w1_sb")
        nc.sync.dma_start(w1_sb[:], w1.rearrange("c (p k) -> c p k", k=FB))
        w2_sb = held.tile([P, FB, C], BF16, name="w2_sb")
        nc.sync.dma_start(w2_sb[:], w2.rearrange("(p k) c -> p k c", k=FB))
        offsets = held.tile([P, N // 16], U16, name="offsets")
        nc.sync.dma_start(offsets[:], offs)
        window = held.tile([C, S], F32, name="window")
        nc.sync.dma_start(window[:], base)

        h_bf = held.tile([C, N], BF16, name="h_bf")
        for j in range(0, N, HALF):
            nc.vector.tensor_copy(h_bf[:, j : j + HALF], h_f32[:, j : j + HALF])

        hid_bf = [held.tile([P, N], BF16, name=f"hid_bf{k}") for k in range(FB)]

        def relu_of_product(k, start, end, matmul_width):
            hid_ps = psum.tile([P, end - start], BF16, name=f"hid_ps{k}_{start}")
            for j in range(start, end, matmul_width):
                nc.tensor.matmul(
                    hid_ps[:, j - start : j - start + matmul_width],
                    w1_sb[:, :, k],
                    h_bf[:, j : j + matmul_width],
                    start=True,
                    stop=True,
                )
            nc.vector.tensor_scalar_max(hid_bf[k][:, start:end], hid_ps[:], 0.0)

        relu_of_product(0, 0, N, HALF)
        relu_of_product(1, 0, N, N)
        for t in range(2):
            for k in range(2, FB):
                relu_of_product(k, t * HALF, (t + 1) * HALF, HALF)

        u_ps = [psum.tile([C, HALF], F32, name=f"u_ps{t}") for t in range(2)]

        def add_block(k, t):
            nc.tensor.matmul(
                u_ps[t][:],
                w2_sb[:, k, :],
                hid_bf[k][:, t * HALF : (t + 1) * HALF],
                start=(k == 0),
                stop=(k == FB - 1),
            )

        for k in range(2):
            for t in range(2):
                add_block(k, t)
        for t in range(2):
            for k in range(2, FB):
                add_block(k, t)

        u_sb = held.tile([C, N], F32, name="u_sb")
        for t in range(2):
            nc.vector.tensor_scalar_mul(u_sb[:, t * HALF : (t + 1) * HALF], u_ps[t][:], RW)

        nc.vector.tensor_tensor(window[:].indirect(offsets[:]), h_f32[:], u_sb[:], ALU.add)
        nc.sync.dma_start(out, window[:])
